import numpy as np
import ml_dtypes


def mxq(x, axis, fmt="e4m3"):
    dtype, down = {"e4m3": (ml_dtypes.float8_e4m3fn, 7), "e5m2": (ml_dtypes.float8_e5m2, 14)}[fmt]
    v = np.moveaxis(np.asarray(x, np.float32).astype(ml_dtypes.bfloat16).astype(np.float64), axis, -1)
    blocks = v.reshape(v.shape[:-1] + (-1, 32))
    amax = np.abs(blocks).max(-1, keepdims=True)
    byte = np.maximum(np.where(amax > 0, np.frexp(amax)[1] - 1 + 127, 0) - down, 1)
    scale = np.exp2(byte - 127.0)
    codes = (blocks / scale).astype(np.float32).astype(dtype).astype(np.float64)
    return np.moveaxis((codes * scale).reshape(v.shape), -1, axis)


WIDE = False


def mx_kscale(k):
    if not WIDE:
        return np.ones(k)
    levels = np.array([10, -10, 5, -5, 0])
    a = np.random.permutation(np.resize(levels, k // 512 * 4)).reshape(k // 512, 4)
    idx = np.arange(k)
    return np.exp2(a[idx // 512, idx % 128 // 32])


BF16 = ml_dtypes.bfloat16


def bf(x):
    return np.asarray(x, np.float32).astype(BF16)


def f64(x):
    return np.asarray(x).astype(np.float64)


B, C, MID, HH, WW = 4, 256, 1024, 32, 32
N = HH * WW


def setup_inputs():
    s, t = mx_kscale(N), mx_kscale(MID)
    a = np.exp(1.5 * np.random.standard_normal((B, N, N)))
    a = a / a.sum(-1, keepdims=True)
    return {
        "attn": bf(a * s),
        "h_x": bf(np.random.standard_normal((B, MID, N)) * 2.0 * t[:, None] / s),
        "v_w": bf(np.random.standard_normal((C, MID)) * 3.0 / np.sqrt(MID) / t),
        "v_b": bf(np.random.standard_normal(C) * 0.3),
        "x": bf(np.random.standard_normal((B, C, HH, WW))),
    }


def reference(attn, h_x, v_w, v_b, x):
    z = mxq(f64(h_x), 2, "e4m3") @ mxq(f64(attn), 2, "e4m3").transpose(0, 2, 1)
    y = (mxq(f64(v_w), 1, "e4m3") @ mxq(z, 1, "e4m3")) + f64(v_b)[None, :, None]
    return y.reshape(B, C, HH, WW) + f64(x)

@@ -1,0 +1,244 @@
+from contextlib import ExitStack
+
+import concourse.mybir as mybir
+from concourse.masks import make_identity
+
+F32 = mybir.dt.float32
+BF16 = mybir.dt.bfloat16
+U32 = mybir.dt.uint32
+U8 = mybir.dt.uint8
+FP8X4 = mybir.dt.float8_e4m3fn_x4
+ADD = mybir.AluOpType.add
+
+B, C, MID, N = 4, 256, 1024, 1024
+P = 128
+PACK = 4
+K_PASS = P * PACK
+PASSES = N // K_PASS
+PAIRS = PACK // 2
+SLAB = 512
+TILES = SLAB // P
+SLABS_PER_BATCH = (N + MID) // SLAB
+ROUNDS_PER_BATCH = (N // SLAB) * (MID // SLAB)
+C_TILES = C // P
+SLABS = B * SLABS_PER_BATCH
+ROUNDS = B * ROUNDS_PER_BATCH
+UNITS = B * (N // SLAB) * C_TILES
+RAW_BUFS = 8
+AHEAD = 2
+
+FLOPS = 2 * B * (MID * N * N + C * MID * N)
+
+
+def tile_soablock_pb_t_kernel(tc, attn, h_x, v_w, v_b, x, out):
+    nc = tc.nc
+    x_rows = x.rearrange("b c h w -> b c (h w)")
+    out_rows = out.rearrange("b c h w -> b c (h w)")
+
+    with ExitStack() as ctx:
+        const = ctx.enter_context(tc.tile_pool(name="const", bufs=1))
+        raw_pool = ctx.enter_context(tc.tile_pool(name="raw", bufs=RAW_BUFS))
+        grouped_pool = ctx.enter_context(tc.tile_pool(name="grouped", bufs=2))
+        slab_pool = ctx.enter_context(tc.tile_pool(name="slab", bufs=SLABS_PER_BATCH))
+        z_pool = ctx.enter_context(tc.tile_pool(name="z", bufs=2))
+        x_pool = ctx.enter_context(tc.tile_pool(name="x", bufs=B))
+        result_pool = ctx.enter_context(tc.tile_pool(name="result", bufs=4))
+        square_pool = ctx.enter_context(tc.psum_pool(name="squares", bufs=4))
+        sum_pool = ctx.enter_context(tc.psum_pool(name="sums", bufs=4))
+        ctx.enter_context(tc.manual_schedule())
+
+        raw_of = {}
+        grouped_of = {}
+        codes_of = {}
+        x_of = {}
+        z_grouped_of = {}
+        z_codes_of = {}
+        y_of = {}
+
+        def slab_rows(s):
+            b, place = divmod(s, SLABS_PER_BATCH)
+            if place == 0:
+                return attn[b, 0:SLAB, :].rearrange("(r p) m -> p r m", p=P)
+            if place == 3:
+                return attn[b, SLAB:N, :].rearrange("(r p) m -> p r m", p=P)
+            first = (place - 1) * SLAB
+            return h_x[b, first : first + SLAB, :].rearrange("(p t) m -> p t m", t=TILES)
+
+        def load_slab(s):
+            raw = raw_pool.tile([P, TILES * N], BF16)
+            nc.sync.dma_start(out=raw[:].rearrange("p (r m) -> p r m", r=TILES), in_=slab_rows(s))
+            raw_of[s] = raw
+            b, place = divmod(s, SLABS_PER_BATCH)
+            if place == SLABS_PER_BATCH - 1:
+                residual = x_pool.tile([P, C_TILES, N], BF16)
+                nc.sync.dma_start(out=residual[:], in_=x_rows[b].rearrange("(a p) n -> p a n", p=P))
+                x_of[b] = residual
+
+        def transpose_slab(s):
+            words = raw_of[s][:].bitcast(F32)
+            grouped = grouped_pool.tile([P, TILES * PASSES * P * PACK], BF16, align_bytes=64)
+            grouped_words = grouped[:].bitcast(F32).rearrange(
+                "p (r k c u) -> p r k c u", r=TILES, k=PASSES, u=PAIRS
+            )
+            for r in range(TILES):
+                bank = square_pool.tile([P, PASSES, PAIRS, P], F32, tag="bank")
+                for k in range(PASSES):
+                    for u in range(PAIRS):
+                        first = ((r * PASSES + k) * PAIRS + u) * P
+                        nc.tensor.transpose(
+                            out=bank[:, k, u, :], in_=words[:, first : first + P], identity=ident_f32[:]
+                        )
+                regrouped = bank[:].rearrange("p k u c -> p k c u")
+                if r % 2 == 0:
+                    nc.scalar.copy(out=grouped_words[:, r, :, :, :], in_=regrouped)
+                else:
+                    nc.vector.tensor_copy(out=grouped_words[:, r, :, :, :], in_=regrouped)
+            grouped_of[s] = grouped
+            if s + RAW_BUFS < SLABS:
+                load_slab(s + RAW_BUFS)
+
+        def quantise_slab(s):
+            codes = slab_pool.tile([P, TILES, PASSES, P], U32, align_bytes=64)
+            scales = slab_pool.tile([P, TILES, PASSES, P], U8, align_bytes=64)
+            nc.vector.quantize_mx(
+                out=codes[:].rearrange("p r k c -> p (r k c)").bitcast(FP8X4),
+                scales=scales[:].rearrange("p r k c -> p (r k c)"),
+                in_=grouped_of[s][:],
+            )
+            codes_of[s] = (codes, scales)
+
+        def mix_positions(j):
+            b, place = divmod(j, ROUNDS_PER_BATCH)
+            half, g = divmod(place, MID // SLAB)
+            a_codes, a_scales = codes_of[b * SLABS_PER_BATCH + 3 * half]
+            h_codes, h_scales = codes_of[b * SLABS_PER_BATCH + 1 + g]
+            z_grouped = z_pool.tile([P, TILES, P, PACK], BF16, align_bytes=64)
+            for r in range(TILES):
+                z_bank = sum_pool.tile([P, PACK, P], F32, tag="sums")
+                for t in range(PACK):
+                    for k in range(PASSES):
+                        nc.tensor.matmul_mx(
+                            out=z_bank[:, t, :],
+                            lhsT=h_codes[:, t, k, :].bitcast(FP8X4),
+                            lhsT_scale=h_scales[:, t, k, :],
+                            rhs=a_codes[:, r, k, :].bitcast(FP8X4),
+                            rhs_scale=a_scales[:, r, k, :],
+                            start=(k == 0),
+                            stop=(k == PASSES - 1),
+                        )
+                nc.scalar.copy(out=z_grouped[:, r, :, :], in_=z_bank[:].rearrange("p t n -> p n t"))
+            z_grouped_of[j] = z_grouped
+
+        def quantise_z(j):
+            b, place = divmod(j, ROUNDS_PER_BATCH)
+            half, g = divmod(place, MID // SLAB)
+            if g == 0:
+                z_codes = z_pool.tile([P, PASSES, SLAB], U32, align_bytes=64)
+                z_scales = z_pool.tile([P, PASSES, SLAB], U8, align_bytes=64)
+                z_codes_of[(b, half)] = (z_codes, z_scales)
+            z_codes, z_scales = z_codes_of[(b, half)]
+            nc.vector.quantize_mx(
+                out=z_codes[:, g, :].bitcast(FP8X4),
+                scales=z_scales[:, g, :],
+                in_=z_grouped_of[j][:].rearrange("p r n t -> p (r n t)"),
+            )
+
+        def map_channels(i):
+            b, place = divmod(i, UNITS // B)
+            half, a = divmod(place, C_TILES)
+            z_codes, z_scales = z_codes_of[(b, half)]
+            o_cols = slice(a * P, (a + 1) * P)
+            y_bank = sum_pool.tile([P, SLAB], F32, tag="sums")
+            for g in range(PASSES):
+                nc.tensor.matmul_mx(
+                    out=y_bank[:],
+                    lhsT=w_codes[:, g, o_cols].bitcast(FP8X4),
+                    lhsT_scale=w_scales[:, g, o_cols],
+                    rhs=z_codes[:, g, :].bitcast(FP8X4),
+                    rhs_scale=z_scales[:, g, :],
+                    start=(g == 0),
+                    stop=(g == PASSES - 1),
+                )
+            y_of[i] = y_bank
+
+        def finish(i):
+            b, place = divmod(i, UNITS // B)
+            half, a = divmod(place, C_TILES)
+            n_cols = slice(half * SLAB, (half + 1) * SLAB)
+            result = result_pool.tile([P, SLAB], F32)
+            nc.vector.scalar_tensor_tensor(
+                out=result[:],
+                in0=y_of[i][:],
+                scalar=bias[:, a : a + 1],
+                in1=x_of[b][:, a, n_cols],
+                op0=ADD,
+                op1=ADD,
+            )
+            nc.sync.dma_start(out=out_rows[b, a * P : (a + 1) * P, n_cols], in_=result[:])
+
+        ident_f32 = const.tile([P, P], F32)
+        make_identity(nc, ident_f32[:])
+        ident_bf16 = const.tile([P, P], BF16)
+        make_identity(nc, ident_bf16[:])
+        bias_rows = const.tile([P, P], BF16)
+        nc.vector.memset(bias_rows[:], 0.0)
+
+        load_slab(0)
+        load_slab(1)
+        w_raw = const.tile([P, C_TILES * MID], BF16)
+        nc.sync.dma_start(
+            out=w_raw[:].rearrange("p (a c) -> p a c", a=C_TILES),
+            in_=v_w.rearrange("(a p) c -> p a c", p=P),
+        )
+        nc.sync.dma_start(out=bias_rows[0:C_TILES, :], in_=v_b.rearrange("(a o) -> a o", a=C_TILES))
+        for s in range(2, RAW_BUFS):
+            load_slab(s)
+
+        for s in range(AHEAD):
+            transpose_slab(s)
+            quantise_slab(s)
+
+        w_words = w_raw[:].bitcast(F32).rearrange(
+            "o (a g p u) -> o a g p u", a=C_TILES, g=PASSES, u=PAIRS
+        )
+        w_grouped = const.tile([P, PASSES * C * PACK], BF16, align_bytes=64)
+        w_grouped_words = w_grouped[:].bitcast(F32).rearrange(
+            "p (g a o u) -> p g a o u", g=PASSES, a=C_TILES, u=PAIRS
+        )
+        for a in range(C_TILES):
+            bank = square_pool.tile([P, PASSES, PAIRS, P], F32, tag="bank")
+            for g in range(PASSES):
+                for u in range(PAIRS):
+                    nc.tensor.transpose(
+                        out=bank[:, g, u, :], in_=w_words[:, a, g, :, u], identity=ident_f32[:]
+                    )
+            nc.vector.tensor_copy(
+                out=w_grouped_words[:, :, a, :, :], in_=bank[:].rearrange("p g u o -> p g o u")
+            )
+        w_codes = const.tile([P, PASSES, C], U32, align_bytes=64)
+        w_scales = const.tile([P, PASSES, C], U8, align_bytes=64)
+
+        bias_bank = square_pool.tile([P, P], BF16, tag="bank")
+        nc.tensor.transpose(out=bias_bank[:], in_=bias_rows[:], identity=ident_bf16[:])
+        bias = const.tile([P, C_TILES], F32)
+        nc.vector.tensor_copy(out=bias[:], in_=bias_bank[:, 0:C_TILES])
+
+        nc.vector.quantize_mx(
+            out=w_codes[:].rearrange("p g o -> p (g o)").bitcast(FP8X4),
+            scales=w_scales[:].rearrange("p g o -> p (g o)"),
+            in_=w_grouped[:],
+        )
+
+        for j in range(ROUNDS + 3):
+            if 0 <= j - 3:
+                finish(j - 3)
+            if j + AHEAD < SLABS:
+                transpose_slab(j + AHEAD)
+            if 0 <= j - 1 < ROUNDS:
+                quantise_z(j - 1)
+            if j + AHEAD < SLABS:
+                quantise_slab(j + AHEAD)
+            if j < ROUNDS:
+                mix_positions(j)
+            if 0 <= j - 2 < UNITS:
+                map_channels(j - 2)

@@ -26,6 +26,8 @@ ROUNDS = B * ROUNDS_PER_BATCH
 UNITS = B * (N // SLAB) * C_TILES
 RAW_BUFS = 8
 AHEAD = 2
+RUN_SLABS = 4
+assert RUN_SLABS >= AHEAD and SLABS % RUN_SLABS == 0
 
 FLOPS = 2 * B * (MID * N * N + C * MID * N)
 
@@ -38,10 +40,10 @@ def tile_soablock_pb_t_kernel(tc, attn, h_x, v_w, v_b, x, out):
     with ExitStack() as ctx:
         const = ctx.enter_context(tc.tile_pool(name="const", bufs=1))
         raw_pool = ctx.enter_context(tc.tile_pool(name="raw", bufs=RAW_BUFS))
-        grouped_pool = ctx.enter_context(tc.tile_pool(name="grouped", bufs=2))
+        grouped_pool = ctx.enter_context(tc.tile_pool(name="grouped", bufs=RUN_SLABS + 1))
         slab_pool = ctx.enter_context(tc.tile_pool(name="slab", bufs=SLABS_PER_BATCH))
         z_pool = ctx.enter_context(tc.tile_pool(name="z", bufs=2))
-        x_pool = ctx.enter_context(tc.tile_pool(name="x", bufs=B))
+        x_pool = ctx.enter_context(tc.tile_pool(name="x", bufs=2))
         result_pool = ctx.enter_context(tc.tile_pool(name="result", bufs=4))
         square_pool = ctx.enter_context(tc.psum_pool(name="squares", bufs=4))
         sum_pool = ctx.enter_context(tc.psum_pool(name="sums", bufs=4))
@@ -68,11 +70,11 @@ def tile_soablock_pb_t_kernel(tc, attn, h_x, v_w, v_b, x, out):
             raw = raw_pool.tile([P, TILES * N], BF16)
             nc.sync.dma_start(out=raw[:].rearrange("p (r m) -> p r m", r=TILES), in_=slab_rows(s))
             raw_of[s] = raw
-            b, place = divmod(s, SLABS_PER_BATCH)
-            if place == SLABS_PER_BATCH - 1:
-                residual = x_pool.tile([P, C_TILES, N], BF16)
-                nc.sync.dma_start(out=residual[:], in_=x_rows[b].rearrange("(a p) n -> p a n", p=P))
-                x_of[b] = residual
+
+        def load_residual(b):
+            residual = x_pool.tile([P, C_TILES, N], BF16)
+            nc.sync.dma_start(out=residual[:], in_=x_rows[b].rearrange("(a p) n -> p a n", p=P))
+            x_of[b] = residual
 
         def transpose_slab(s):
             words = raw_of[s][:].bitcast(F32)
@@ -183,20 +185,15 @@ def tile_soablock_pb_t_kernel(tc, attn, h_x, v_w, v_b, x, out):
         bias_rows = const.tile([P, P], BF16)
         nc.vector.memset(bias_rows[:], 0.0)
 
-        load_slab(0)
-        load_slab(1)
         w_raw = const.tile([P, C_TILES * MID], BF16)
         nc.sync.dma_start(
             out=w_raw[:].rearrange("p (a c) -> p a c", a=C_TILES),
             in_=v_w.rearrange("(a p) c -> p a c", p=P),
         )
         nc.sync.dma_start(out=bias_rows[0:C_TILES, :], in_=v_b.rearrange("(a o) -> a o", a=C_TILES))
-        for s in range(2, RAW_BUFS):
+        for s in range(RAW_BUFS):
             load_slab(s)
-
-        for s in range(AHEAD):
-            transpose_slab(s)
-            quantise_slab(s)
+        load_residual(0)
 
         w_words = w_raw[:].bitcast(F32).rearrange(
             "o (a g p u) -> o a g p u", a=C_TILES, g=PASSES, u=PAIRS
@@ -229,15 +226,23 @@ def tile_soablock_pb_t_kernel(tc, attn, h_x, v_w, v_b, x, out):
             in_=w_grouped[:],
         )
 
+        for s in range(RUN_SLABS):
+            transpose_slab(s)
+            quantise_slab(s)
+
         for j in range(ROUNDS + 3):
+            s = j + AHEAD
             if 0 <= j - 3:
                 finish(j - 3)
-            if j + AHEAD < SLABS:
-                transpose_slab(j + AHEAD)
+            if s < SLABS and s % SLABS_PER_BATCH == 0:
+                load_residual(s // SLABS_PER_BATCH)
+            if RUN_SLABS <= s < SLABS and s % RUN_SLABS == 0:
+                for later in range(RUN_SLABS):
+                    transpose_slab(s + later)
             if 0 <= j - 1 < ROUNDS:
                 quantise_z(j - 1)
-            if j + AHEAD < SLABS:
-                quantise_slab(j + AHEAD)
+            if RUN_SLABS <= s < SLABS:
+                quantise_slab(s)
             if j < ROUNDS:
                 mix_positions(j)
             if 0 <= j - 2 < UNITS:

@@ -24,10 +24,10 @@ C_TILES = C // P
 SLABS = B * SLABS_PER_BATCH
 ROUNDS = B * ROUNDS_PER_BATCH
 UNITS = B * (N // SLAB) * C_TILES
+PART = 2
+PARTS = TILES // PART
 RAW_BUFS = 8
 AHEAD = 2
-RUN_SLABS = 4
-assert RUN_SLABS >= AHEAD and SLABS % RUN_SLABS == 0
 
 FLOPS = 2 * B * (MID * N * N + C * MID * N)
 
@@ -40,10 +40,10 @@ def tile_soablock_pb_t_kernel(tc, attn, h_x, v_w, v_b, x, out):
     with ExitStack() as ctx:
         const = ctx.enter_context(tc.tile_pool(name="const", bufs=1))
         raw_pool = ctx.enter_context(tc.tile_pool(name="raw", bufs=RAW_BUFS))
-        grouped_pool = ctx.enter_context(tc.tile_pool(name="grouped", bufs=RUN_SLABS + 1))
-        slab_pool = ctx.enter_context(tc.tile_pool(name="slab", bufs=SLABS_PER_BATCH))
+        grouped_pool = ctx.enter_context(tc.tile_pool(name="grouped", bufs=2))
+        slab_pool = ctx.enter_context(tc.tile_pool(name="slab", bufs=5))
         z_pool = ctx.enter_context(tc.tile_pool(name="z", bufs=2))
-        x_pool = ctx.enter_context(tc.tile_pool(name="x", bufs=2))
+        x_pool = ctx.enter_context(tc.tile_pool(name="x", bufs=B))
         result_pool = ctx.enter_context(tc.tile_pool(name="result", bufs=4))
         square_pool = ctx.enter_context(tc.psum_pool(name="squares", bufs=4))
         sum_pool = ctx.enter_context(tc.psum_pool(name="sums", bufs=4))
@@ -59,30 +59,42 @@ def tile_soablock_pb_t_kernel(tc, attn, h_x, v_w, v_b, x, out):
 
         def slab_rows(s):
             b, place = divmod(s, SLABS_PER_BATCH)
-            if place == 0:
-                return attn[b, 0:SLAB, :].rearrange("(r p) m -> p r m", p=P)
-            if place == 3:
-                return attn[b, SLAB:N, :].rearrange("(r p) m -> p r m", p=P)
-            first = (place - 1) * SLAB
-            return h_x[b, first : first + SLAB, :].rearrange("(p t) m -> p t m", t=TILES)
+            first = (place // 2) * SLAB
+            if place % 2 == 0:
+                return h_x[b, first : first + SLAB, :].rearrange("(p t) m -> p t m", t=TILES)
+            return attn[b, first : first + SLAB, :].rearrange("(r p) m -> p r m", p=P)
 
         def load_slab(s):
             raw = raw_pool.tile([P, TILES * N], BF16)
-            nc.sync.dma_start(out=raw[:].rearrange("p (r m) -> p r m", r=TILES), in_=slab_rows(s))
+            raw_tiles = raw[:].rearrange("p (r m) -> p r m", r=TILES)
+            if s < AHEAD:
+                for r in range(TILES):
+                    nc.sync.dma_start(out=raw_tiles[:, r, :], in_=slab_rows(s)[:, r, :])
+            else:
+                nc.sync.dma_start(out=raw_tiles, in_=slab_rows(s))
             raw_of[s] = raw
+            b, place = divmod(s, SLABS_PER_BATCH)
+            if place == SLABS_PER_BATCH - 1:
+                residual = x_pool.tile([P, C_TILES, N], BF16)
+                nc.sync.dma_start(out=residual[:], in_=x_rows[b].rearrange("(a p) n -> p a n", p=P))
+                x_of[b] = residual
 
-        def load_residual(b):
-            residual = x_pool.tile([P, C_TILES, N], BF16)
-            nc.sync.dma_start(out=residual[:], in_=x_rows[b].rearrange("(a p) n -> p a n", p=P))
-            x_of[b] = residual
+        def open_slab(s):
+            grouped = grouped_pool.tile([P, TILES, PASSES * P * PACK], BF16, align_bytes=64)
+            codes = slab_pool.tile([P, TILES, PASSES, P], U32, align_bytes=64)
+            scales = slab_pool.tile([P, TILES, PASSES, P], U8, align_bytes=64)
+            grouped_of[s] = grouped
+            codes_of[s] = (codes, scales)
 
-        def transpose_slab(s):
+        def transpose_part(s, part):
             words = raw_of[s][:].bitcast(F32)
-            grouped = grouped_pool.tile([P, TILES * PASSES * P * PACK], BF16, align_bytes=64)
-            grouped_words = grouped[:].bitcast(F32).rearrange(
-                "p (r k c u) -> p r k c u", r=TILES, k=PASSES, u=PAIRS
+            grouped_words = (
+                grouped_of[s][:]
+                .rearrange("p r v -> p (r v)")
+                .bitcast(F32)
+                .rearrange("p (r k c u) -> p r k c u", r=TILES, k=PASSES, u=PAIRS)
             )
-            for r in range(TILES):
+            for r in range(part * PART, (part + 1) * PART):
                 bank = square_pool.tile([P, PASSES, PAIRS, P], F32, tag="bank")
                 for k in range(PASSES):
                     for u in range(PAIRS):
@@ -95,25 +107,23 @@ def tile_soablock_pb_t_kernel(tc, attn, h_x, v_w, v_b, x, out):
                     nc.scalar.copy(out=grouped_words[:, r, :, :, :], in_=regrouped)
                 else:
                     nc.vector.tensor_copy(out=grouped_words[:, r, :, :, :], in_=regrouped)
-            grouped_of[s] = grouped
-            if s + RAW_BUFS < SLABS:
+            if part == PARTS - 1 and s + RAW_BUFS < SLABS:
                 load_slab(s + RAW_BUFS)
 
-        def quantise_slab(s):
-            codes = slab_pool.tile([P, TILES, PASSES, P], U32, align_bytes=64)
-            scales = slab_pool.tile([P, TILES, PASSES, P], U8, align_bytes=64)
+        def quantise_part(s, part):
+            codes, scales = codes_of[s]
+            tiles = slice(part * PART, (part + 1) * PART)
             nc.vector.quantize_mx(
-                out=codes[:].rearrange("p r k c -> p (r k c)").bitcast(FP8X4),
-                scales=scales[:].rearrange("p r k c -> p (r k c)"),
-                in_=grouped_of[s][:],
+                out=codes[:, tiles, :, :].rearrange("p r k c -> p (r k c)").bitcast(FP8X4),
+                scales=scales[:, tiles, :, :].rearrange("p r k c -> p (r k c)"),
+                in_=grouped_of[s][:, tiles, :].rearrange("p r v -> p (r v)"),
             )
-            codes_of[s] = (codes, scales)
 
         def mix_positions(j):
             b, place = divmod(j, ROUNDS_PER_BATCH)
             half, g = divmod(place, MID // SLAB)
-            a_codes, a_scales = codes_of[b * SLABS_PER_BATCH + 3 * half]
-            h_codes, h_scales = codes_of[b * SLABS_PER_BATCH + 1 + g]
+            h_codes, h_scales = codes_of[b * SLABS_PER_BATCH + 2 * g]
+            a_codes, a_scales = codes_of[b * SLABS_PER_BATCH + 2 * half + 1]
             z_grouped = z_pool.tile([P, TILES, P, PACK], BF16, align_bytes=64)
             for r in range(TILES):
                 z_bank = sum_pool.tile([P, PACK, P], F32, tag="sums")
@@ -185,15 +195,28 @@ def tile_soablock_pb_t_kernel(tc, attn, h_x, v_w, v_b, x, out):
         bias_rows = const.tile([P, P], BF16)
         nc.vector.memset(bias_rows[:], 0.0)
 
+        for s in range(AHEAD + 1):
+            load_slab(s)
         w_raw = const.tile([P, C_TILES * MID], BF16)
         nc.sync.dma_start(
             out=w_raw[:].rearrange("p (a c) -> p a c", a=C_TILES),
             in_=v_w.rearrange("(a p) c -> p a c", p=P),
         )
         nc.sync.dma_start(out=bias_rows[0:C_TILES, :], in_=v_b.rearrange("(a o) -> a o", a=C_TILES))
-        for s in range(RAW_BUFS):
+        for s in range(AHEAD + 1, RAW_BUFS):
             load_slab(s)
-        load_residual(0)
+
+        for s in range(AHEAD):
+            open_slab(s)
+            for part in range(PARTS):
+                transpose_part(s, part)
+                quantise_part(s, part)
+        mix_positions(0)
+        open_slab(AHEAD)
+        for part in range(PARTS):
+            transpose_part(AHEAD, part)
+        for part in range(PARTS):
+            quantise_part(AHEAD, part)
 
         w_words = w_raw[:].bitcast(F32).rearrange(
             "o (a g p u) -> o a g p u", a=C_TILES, g=PASSES, u=PAIRS
@@ -226,23 +249,18 @@ def tile_soablock_pb_t_kernel(tc, attn, h_x, v_w, v_b, x, out):
             in_=w_grouped[:],
         )
 
-        for s in range(RUN_SLABS):
-            transpose_slab(s)
-            quantise_slab(s)
-
-        for j in range(ROUNDS + 3):
-            s = j + AHEAD
+        for j in range(1, ROUNDS + 3):
             if 0 <= j - 3:
                 finish(j - 3)
-            if s < SLABS and s % SLABS_PER_BATCH == 0:
-                load_residual(s // SLABS_PER_BATCH)
-            if RUN_SLABS <= s < SLABS and s % RUN_SLABS == 0:
-                for later in range(RUN_SLABS):
-                    transpose_slab(s + later)
-            if 0 <= j - 1 < ROUNDS:
+            if j + AHEAD < SLABS:
+                open_slab(j + AHEAD)
+                for part in range(PARTS):
+                    transpose_part(j + AHEAD, part)
+            if j - 1 < ROUNDS:
                 quantise_z(j - 1)
-            if RUN_SLABS <= s < SLABS:
-                quantise_slab(s)
+            if j + AHEAD < SLABS:
+                for part in range(PARTS):
+                    quantise_part(j + AHEAD, part)
             if j < ROUNDS:
                 mix_positions(j)
             if 0 <= j - 2 < UNITS:

from contextlib import ExitStack

import concourse.mybir as mybir
from concourse.masks import make_identity

F32 = mybir.dt.float32
BF16 = mybir.dt.bfloat16
U32 = mybir.dt.uint32
U8 = mybir.dt.uint8
FP8X4 = mybir.dt.float8_e4m3fn_x4
ADD = mybir.AluOpType.add

B, C, MID, N = 4, 256, 1024, 1024
P = 128
PACK = 4
K_PASS = P * PACK
PASSES = N // K_PASS
PAIRS = PACK // 2
SLAB = 512
TILES = SLAB // P
SLABS_PER_BATCH = (N + MID) // SLAB
ROUNDS_PER_BATCH = (N // SLAB) * (MID // SLAB)
C_TILES = C // P
SLABS = B * SLABS_PER_BATCH
ROUNDS = B * ROUNDS_PER_BATCH
UNITS = B * (N // SLAB) * C_TILES
PART = 2
PARTS = TILES // PART
RAW_BUFS = 8
AHEAD = 2

FLOPS = 2 * B * (MID * N * N + C * MID * N)


def tile_soablock_pb_t_kernel(tc, attn, h_x, v_w, v_b, x, out):
    nc = tc.nc
    x_rows = x.rearrange("b c h w -> b c (h w)")
    out_rows = out.rearrange("b c h w -> b c (h w)")

    with ExitStack() as ctx:
        const = ctx.enter_context(tc.tile_pool(name="const", bufs=1))
        raw_pool = ctx.enter_context(tc.tile_pool(name="raw", bufs=RAW_BUFS))
        grouped_pool = ctx.enter_context(tc.tile_pool(name="grouped", bufs=2))
        slab_pool = ctx.enter_context(tc.tile_pool(name="slab", bufs=5))
        z_pool = ctx.enter_context(tc.tile_pool(name="z", bufs=2))
        x_pool = ctx.enter_context(tc.tile_pool(name="x", bufs=B))
        result_pool = ctx.enter_context(tc.tile_pool(name="result", bufs=4))
        square_pool = ctx.enter_context(tc.psum_pool(name="squares", bufs=4))
        sum_pool = ctx.enter_context(tc.psum_pool(name="sums", bufs=4))
        ctx.enter_context(tc.manual_schedule())

        raw_of = {}
        grouped_of = {}
        codes_of = {}
        x_of = {}
        z_grouped_of = {}
        z_codes_of = {}
        y_of = {}

        def slab_rows(s):
            b, place = divmod(s, SLABS_PER_BATCH)
            first = (place // 2) * SLAB
            if place % 2 == 0:
                return h_x[b, first : first + SLAB, :].rearrange("(p t) m -> p t m", t=TILES)
            return attn[b, first : first + SLAB, :].rearrange("(r p) m -> p r m", p=P)

        def load_slab(s):
            raw = raw_pool.tile([P, TILES * N], BF16)
            raw_tiles = raw[:].rearrange("p (r m) -> p r m", r=TILES)
            if s < AHEAD:
                for r in range(TILES):
                    nc.sync.dma_start(out=raw_tiles[:, r, :], in_=slab_rows(s)[:, r, :])
            else:
                nc.sync.dma_start(out=raw_tiles, in_=slab_rows(s))
            raw_of[s] = raw
            b, place = divmod(s, SLABS_PER_BATCH)
            if place == SLABS_PER_BATCH - 1:
                residual = x_pool.tile([P, C_TILES, N], BF16)
                nc.sync.dma_start(out=residual[:], in_=x_rows[b].rearrange("(a p) n -> p a n", p=P))
                x_of[b] = residual

        def open_slab(s):
            grouped = grouped_pool.tile([P, TILES, PASSES * P * PACK], BF16, align_bytes=64)
            codes = slab_pool.tile([P, TILES, PASSES, P], U32, align_bytes=64)
            scales = slab_pool.tile([P, TILES, PASSES, P], U8, align_bytes=64)
            grouped_of[s] = grouped
            codes_of[s] = (codes, scales)

        def transpose_part(s, part):
            words = raw_of[s][:].bitcast(F32)
            grouped_words = (
                grouped_of[s][:]
                .rearrange("p r v -> p (r v)")
                .bitcast(F32)
                .rearrange("p (r k c u) -> p r k c u", r=TILES, k=PASSES, u=PAIRS)
            )
            for r in range(part * PART, (part + 1) * PART):
                bank = square_pool.tile([P, PASSES, PAIRS, P], F32, tag="bank")
                for k in range(PASSES):
                    for u in range(PAIRS):
                        first = ((r * PASSES + k) * PAIRS + u) * P
                        nc.tensor.transpose(
                            out=bank[:, k, u, :], in_=words[:, first : first + P], identity=ident_f32[:]
                        )
                regrouped = bank[:].rearrange("p k u c -> p k c u")
                if r % 2 == 0:
                    nc.scalar.copy(out=grouped_words[:, r, :, :, :], in_=regrouped)
                else:
                    nc.vector.tensor_copy(out=grouped_words[:, r, :, :, :], in_=regrouped)
            if part == PARTS - 1 and s + RAW_BUFS < SLABS:
                load_slab(s + RAW_BUFS)

        def quantise_part(s, part):
            codes, scales = codes_of[s]
            tiles = slice(part * PART, (part + 1) * PART)
            nc.vector.quantize_mx(
                out=codes[:, tiles, :, :].rearrange("p r k c -> p (r k c)").bitcast(FP8X4),
                scales=scales[:, tiles, :, :].rearrange("p r k c -> p (r k c)"),
                in_=grouped_of[s][:, tiles, :].rearrange("p r v -> p (r v)"),
            )

        def mix_positions(j):
            b, place = divmod(j, ROUNDS_PER_BATCH)
            half, g = divmod(place, MID // SLAB)
            h_codes, h_scales = codes_of[b * SLABS_PER_BATCH + 2 * g]
            a_codes, a_scales = codes_of[b * SLABS_PER_BATCH + 2 * half + 1]
            z_grouped = z_pool.tile([P, TILES, P, PACK], BF16, align_bytes=64)
            for r in range(TILES):
                z_bank = sum_pool.tile([P, PACK, P], F32, tag="sums")
                for t in range(PACK):
                    for k in range(PASSES):
                        nc.tensor.matmul_mx(
                            out=z_bank[:, t, :],
                            lhsT=h_codes[:, t, k, :].bitcast(FP8X4),
                            lhsT_scale=h_scales[:, t, k, :],
                            rhs=a_codes[:, r, k, :].bitcast(FP8X4),
                            rhs_scale=a_scales[:, r, k, :],
                            start=(k == 0),
                            stop=(k == PASSES - 1),
                        )
                nc.scalar.copy(out=z_grouped[:, r, :, :], in_=z_bank[:].rearrange("p t n -> p n t"))
            z_grouped_of[j] = z_grouped

        def quantise_z(j):
            b, place = divmod(j, ROUNDS_PER_BATCH)
            half, g = divmod(place, MID // SLAB)
            if g == 0:
                z_codes = z_pool.tile([P, PASSES, SLAB], U32, align_bytes=64)
                z_scales = z_pool.tile([P, PASSES, SLAB], U8, align_bytes=64)
                z_codes_of[(b, half)] = (z_codes, z_scales)
            z_codes, z_scales = z_codes_of[(b, half)]
            nc.vector.quantize_mx(
                out=z_codes[:, g, :].bitcast(FP8X4),
                scales=z_scales[:, g, :],
                in_=z_grouped_of[j][:].rearrange("p r n t -> p (r n t)"),
            )

        def map_channels(i):
            b, place = divmod(i, UNITS // B)
            half, a = divmod(place, C_TILES)
            z_codes, z_scales = z_codes_of[(b, half)]
            o_cols = slice(a * P, (a + 1) * P)
            y_bank = sum_pool.tile([P, SLAB], F32, tag="sums")
            for g in range(PASSES):
                nc.tensor.matmul_mx(
                    out=y_bank[:],
                    lhsT=w_codes[:, g, o_cols].bitcast(FP8X4),
                    lhsT_scale=w_scales[:, g, o_cols],
                    rhs=z_codes[:, g, :].bitcast(FP8X4),
                    rhs_scale=z_scales[:, g, :],
                    start=(g == 0),
                    stop=(g == PASSES - 1),
                )
            y_of[i] = y_bank

        def finish(i):
            b, place = divmod(i, UNITS // B)
            half, a = divmod(place, C_TILES)
            n_cols = slice(half * SLAB, (half + 1) * SLAB)
            result = result_pool.tile([P, SLAB], F32)
            nc.vector.scalar_tensor_tensor(
                out=result[:],
                in0=y_of[i][:],
                scalar=bias[:, a : a + 1],
                in1=x_of[b][:, a, n_cols],
                op0=ADD,
                op1=ADD,
            )
            nc.sync.dma_start(out=out_rows[b, a * P : (a + 1) * P, n_cols], in_=result[:])

        ident_f32 = const.tile([P, P], F32)
        make_identity(nc, ident_f32[:])
        ident_bf16 = const.tile([P, P], BF16)
        make_identity(nc, ident_bf16[:])
        bias_rows = const.tile([P, P], BF16)
        nc.vector.memset(bias_rows[:], 0.0)

        for s in range(AHEAD + 1):
            load_slab(s)
        w_raw = const.tile([P, C_TILES * MID], BF16)
        nc.sync.dma_start(
            out=w_raw[:].rearrange("p (a c) -> p a c", a=C_TILES),
            in_=v_w.rearrange("(a p) c -> p a c", p=P),
        )
        nc.sync.dma_start(out=bias_rows[0:C_TILES, :], in_=v_b.rearrange("(a o) -> a o", a=C_TILES))
        for s in range(AHEAD + 1, RAW_BUFS):
            load_slab(s)

        for s in range(AHEAD):
            open_slab(s)
            for part in range(PARTS):
                transpose_part(s, part)
                quantise_part(s, part)
        mix_positions(0)
        open_slab(AHEAD)
        for part in range(PARTS):
            transpose_part(AHEAD, part)
        for part in range(PARTS):
            quantise_part(AHEAD, part)

        w_words = w_raw[:].bitcast(F32).rearrange(
            "o (a g p u) -> o a g p u", a=C_TILES, g=PASSES, u=PAIRS
        )
        w_grouped = const.tile([P, PASSES * C * PACK], BF16, align_bytes=64)
        w_grouped_words = w_grouped[:].bitcast(F32).rearrange(
            "p (g a o u) -> p g a o u", g=PASSES, a=C_TILES, u=PAIRS
        )
        for a in range(C_TILES):
            bank = square_pool.tile([P, PASSES, PAIRS, P], F32, tag="bank")
            for g in range(PASSES):
                for u in range(PAIRS):
                    nc.tensor.transpose(
                        out=bank[:, g, u, :], in_=w_words[:, a, g, :, u], identity=ident_f32[:]
                    )
            nc.vector.tensor_copy(
                out=w_grouped_words[:, :, a, :, :], in_=bank[:].rearrange("p g u o -> p g o u")
            )
        w_codes = const.tile([P, PASSES, C], U32, align_bytes=64)
        w_scales = const.tile([P, PASSES, C], U8, align_bytes=64)

        bias_bank = square_pool.tile([P, P], BF16, tag="bank")
        nc.tensor.transpose(out=bias_bank[:], in_=bias_rows[:], identity=ident_bf16[:])
        bias = const.tile([P, C_TILES], F32)
        nc.vector.tensor_copy(out=bias[:], in_=bias_bank[:, 0:C_TILES])

        nc.vector.quantize_mx(
            out=w_codes[:].rearrange("p g o -> p (g o)").bitcast(FP8X4),
            scales=w_scales[:].rearrange("p g o -> p (g o)"),
            in_=w_grouped[:],
        )

        for j in range(1, ROUNDS + 3):
            if 0 <= j - 3:
                finish(j - 3)
            if j + AHEAD < SLABS:
                open_slab(j + AHEAD)
                for part in range(PARTS):
                    transpose_part(j + AHEAD, part)
            if j - 1 < ROUNDS:
                quantise_z(j - 1)
            if j + AHEAD < SLABS:
                for part in range(PARTS):
                    quantise_part(j + AHEAD, part)
            if j < ROUNDS:
                mix_positions(j)
            if 0 <= j - 2 < UNITS:
                map_channels(j - 2)
